import numpy as np
import ml_dtypes

BF16 = ml_dtypes.bfloat16


def bf(x):
    return np.asarray(x, np.float32).astype(BF16)


def f32(x):
    return np.asarray(x, np.float32)


def f64(x):
    return np.asarray(x).astype(np.float64)


def striped(idx):
    return np.tile(idx.reshape(-1, 16).T, (8, 1))


V, E, NH, DH, B, T, W, N, HALF, K = 4096, 256, 2, 128, 12, 512, 64, 6144, 2048, 3


def setup_inputs():
    return {
        "emb": f32(np.random.standard_normal((E, V))),
        "wq": bf(np.random.standard_normal((E, E)) / np.sqrt(E)),
        "bq": f32(0.1 * np.random.standard_normal((E, 1))),
        "wk": bf(np.random.standard_normal((E, E)) / np.sqrt(E)),
        "wv": bf(2.0 * np.random.standard_normal((E, E)) / np.sqrt(E)),
        "bv": f32(0.1 * np.random.standard_normal((E, 1))),
        "wo": bf(2.0 * np.random.standard_normal((E, E)) / np.sqrt(E)),
        "bo": f32(0.1 * np.random.standard_normal((E, 1))),
        "offs": striped(np.concatenate([np.random.permutation(V)[:HALF] for _ in range(K)])),
    }


def reference(emb, wq, bq, wk, wv, bv, wo, bo, offs):
    idx = offs[:16].T.reshape(-1)
    x = f64(emb)[:, idx]
    query = (f64(wq).T @ x + f64(bq)) / np.sqrt(DH)
    key = f64(wk).T @ x
    value = f64(wv).T @ x + f64(bv)
    pos = np.arange(T)
    band = np.abs(pos[:, None] - pos[None, :]) <= W
    ctx = np.zeros((E, N))
    for seq in range(B):
        cols = slice(seq * T, (seq + 1) * T)
        for head in range(NH):
            rows = slice(head * DH, (head + 1) * DH)
            score = query[rows, cols].T @ key[rows, cols]
            score = np.where(band, score, -np.inf)
            p = np.exp(score - score.max(axis=1, keepdims=True))
            p = p / p.sum(axis=1, keepdims=True)
            ctx[rows, cols] = value[rows, cols] @ p.T
    return f64(wo).T @ ctx + f64(bo)

@@ -1,0 +1,200 @@
+import concourse.mybir as mybir
+from concourse.masks import make_identity
+
+F32, BF16, U16 = mybir.dt.float32, mybir.dt.bfloat16, mybir.dt.uint16
+ACT = mybir.ActivationFunctionType
+ALU = mybir.AluOpType
+
+P = 128
+VOCAB = 4096
+EMBED = 256
+CHUNKS = EMBED // P
+HEADS, HEAD_DIM = 2, 128
+SEQS, SEQ_LEN = 12, 512
+REACH = 64
+TOKENS = SEQS * SEQ_LEN
+PADDED = TOKENS + 2 * REACH
+BLOCKS = SEQ_LEN // P
+SPAN = P + 2 * REACH
+MASKED = -1.0e30
+
+BAND_PAIRS = SEQS * (SEQ_LEN * (2 * REACH + 1) - REACH * (REACH + 1))
+FLOPS = 4 * 2 * EMBED * EMBED * TOKENS + 2 * 2 * HEAD_DIM * HEADS * BAND_PAIRS
+
+
+def tile_textclassifier_b_kernel(tc, emb, wq, bq, wk, wv, bv, wo, bo, offs, out):
+    nc = tc.nc
+    with (
+        tc.tile_pool(name="held", bufs=1) as held,
+        tc.tile_pool(name="work", bufs=4) as work,
+        tc.tile_pool(name="stats", bufs=8) as stats,
+        tc.psum_pool(name="psum", bufs=2) as psum,
+    ):
+        offsets = held.tile([P, TOKENS // 16], U16, name="offsets")
+        nc.sync.dma_start(offsets[:], offs)
+        table = [held.tile([P, VOCAB], F32, name=f"table{c}") for c in range(CHUNKS)]
+        for c in range(CHUNKS):
+            nc.sync.dma_start(table[c][:], emb[c * P : (c + 1) * P, :])
+
+        def load_weight(w, name):
+            tile = held.tile([P, CHUNKS, EMBED], BF16, name=name)
+            nc.scalar.dma_start(tile[:], w.rearrange("(c p) m -> p c m", p=P))
+            return tile
+
+        def load_bias(b, name):
+            tile = held.tile([P, CHUNKS], F32, name=name)
+            with nc.allow_non_contiguous_dma(reason="one value to a partition"):
+                nc.scalar.dma_start(tile[:], b.rearrange("(c p) o -> p (c o)", p=P))
+            return tile
+
+        wq_sb, wk_sb = load_weight(wq, "wq_sb"), load_weight(wk, "wk_sb")
+        wv_sb, wo_sb = load_weight(wv, "wv_sb"), load_weight(wo, "wo_sb")
+        bq_sb, bv_sb, bo_sb = load_bias(bq, "bq_sb"), load_bias(bv, "bv_sb"), load_bias(bo, "bo_sb")
+
+        ident = held.tile([P, P], BF16, name="ident")
+        make_identity(nc, ident[:])
+
+        band = [held.tile([P, SPAN], BF16, name=f"band{b}") for b in range(BLOCKS)]
+        for b in range(BLOCKS):
+            nc.gpsimd.memset(band[b][:], 0.0)
+            nc.gpsimd.affine_select(
+                out=band[b][:], in_=band[b][:], pattern=[[1, SPAN]], compare_op=ALU.is_ge,
+                fill=MASKED, base=0, channel_multiplier=-1,
+            )
+            nc.gpsimd.affine_select(
+                out=band[b][:], in_=band[b][:], pattern=[[-1, SPAN]], compare_op=ALU.is_ge,
+                fill=MASKED, base=2 * REACH, channel_multiplier=1,
+            )
+        nc.gpsimd.memset(band[0][:, 0:REACH], MASKED)
+        nc.gpsimd.memset(band[BLOCKS - 1][:, SPAN - REACH : SPAN], MASKED)
+
+        x_pad = held.tile([P, CHUNKS, PADDED], BF16, name="x_pad")
+        keys = held.tile([P, HEADS, PADDED], BF16, name="keys")
+        for padded in (x_pad, keys):
+            nc.gpsimd.memset(padded[:, :, 0:REACH], 0.0)
+            nc.gpsimd.memset(padded[:, :, PADDED - REACH : PADDED], 0.0)
+        value_blocks = PADDED // P
+        values = held.tile([P, value_blocks, EMBED], BF16, name="values")
+
+        def gather(s):
+            piece = offsets[:, s * (SEQ_LEN // 16) : (s + 1) * (SEQ_LEN // 16)]
+            for c in range(CHUNKS):
+                picked = work.tile([P, SEQ_LEN], F32, name="picked")
+                nc.scalar.activation(picked[:], table[c][:].indirect(piece), ACT.Copy)
+                nc.gpsimd.tensor_scalar(
+                    x_pad[:, c, REACH + s * SEQ_LEN : REACH + (s + 1) * SEQ_LEN], picked[:],
+                    1.0, 0.0, op0=ALU.mult, op1=ALU.add,
+                )
+
+        def project_values(first, count):
+            value_ps = psum.tile([P, 2, EMBED], F32, name="value_ps", tag="proj_ps")
+            for k in range(count):
+                g = first + k
+                for c in range(CHUNKS):
+                    nc.tensor.matmul(
+                        value_ps[:, k, :], x_pad[:, c, g * P : (g + 1) * P], wv_sb[:, c, :],
+                        start=(c == 0), stop=(c == CHUNKS - 1),
+                    )
+            nc.vector.tensor_copy(values[:, first : first + count, :], value_ps[:, 0:count, :])
+
+        def project(s):
+            lo = REACH + s * SEQ_LEN
+            query = work.tile([P, HEADS, SEQ_LEN], BF16, name="query")
+            for h in range(HEADS):
+                query_ps = psum.tile([P, SEQ_LEN], F32, name="query_ps", tag="proj_ps")
+                for c in range(CHUNKS):
+                    nc.tensor.matmul(
+                        query_ps[:], wq_sb[:, c, h * P : (h + 1) * P], x_pad[:, c, lo : lo + SEQ_LEN],
+                        start=(c == 0), stop=(c == CHUNKS - 1),
+                    )
+                nc.vector.tensor_scalar(
+                    query[:, h, :], query_ps[:], bq_sb[:, h : h + 1], HEAD_DIM ** -0.5,
+                    op0=ALU.add, op1=ALU.mult,
+                )
+                key_ps = psum.tile([P, SEQ_LEN], F32, name="key_ps", tag="proj_ps")
+                for c in range(CHUNKS):
+                    nc.tensor.matmul(
+                        key_ps[:], wk_sb[:, c, h * P : (h + 1) * P], x_pad[:, c, lo : lo + SEQ_LEN],
+                        start=(c == 0), stop=(c == CHUNKS - 1),
+                    )
+                nc.scalar.copy(keys[:, h, lo : lo + SEQ_LEN], key_ps[:])
+            for first in range(BLOCKS * s, BLOCKS * (s + 1), 2):
+                project_values(first, 2)
+            return query
+
+        def attend(s, query):
+            ctx = work.tile([P, HEADS, SEQ_LEN], BF16, name="ctx")
+            for h in range(HEADS):
+                ctx_ps = psum.tile([P, SEQ_LEN], F32, name="ctx_ps")
+                for first in range(0, BLOCKS, 2):
+                    score_ps = psum.tile([P, 2, SPAN], F32, name="score_ps")
+                    for k in range(2):
+                        b = first + k
+                        nc.tensor.matmul(score_ps[:, k, :], ident[:], band[b][:], start=True, stop=False)
+                        nc.tensor.matmul(
+                            score_ps[:, k, :], query[:, h, b * P : (b + 1) * P],
+                            keys[:, h, s * SEQ_LEN + b * P : s * SEQ_LEN + b * P + SPAN],
+                            start=False, stop=True,
+                        )
+                    neg_max = stats.tile([P, 2], F32, name="neg_max")
+                    nc.vector.tensor_reduce(
+                        out=neg_max[:], in_=score_ps[:], axis=mybir.AxisListType.X, op=ALU.max, negate=True
+                    )
+                    expo = work.tile([P, 2, SPAN], F32, name="expo")
+                    total = stats.tile([P, 2], F32, name="total")
+                    for k in range(2):
+                        nc.scalar.activation(
+                            expo[:, k, :], score_ps[:, k, :], ACT.Exp,
+                            bias=neg_max[:, k : k + 1], scale=1.0, accum_out=total[:, k : k + 1],
+                        )
+                    inverse = stats.tile([P, 2], F32, name="inverse")
+                    nc.vector.reciprocal(inverse[:], total[:])
+                    prob = work.tile([P, 2, SPAN], BF16, name="prob")
+                    for k in range(2):
+                        nc.gpsimd.tensor_scalar(
+                            prob[:, k, :], expo[:, k, :], inverse[:, k : k + 1], 0.0,
+                            op0=ALU.mult, op1=ALU.add,
+                        )
+                    prob_t_ps = psum.tile([P, 4, P], BF16, name="prob_t_ps")
+                    for k in range(2):
+                        for half in range(2):
+                            nc.tensor.transpose(
+                                prob_t_ps[:, 2 * k + half, :], prob[:, k, half * P : (half + 1) * P], ident[:]
+                            )
+                    prob_t = work.tile([P, 4, P], BF16, name="prob_t")
+                    nc.vector.tensor_copy(prob_t[:], prob_t_ps[:])
+                    for k in range(2):
+                        b = first + k
+                        for half in range(2):
+                            nc.tensor.matmul(
+                                ctx_ps[:, b * P : (b + 1) * P],
+                                values[:, BLOCKS * s + b + half, h * P : (h + 1) * P],
+                                prob_t[:, 2 * k + half, :],
+                                start=(half == 0), stop=(half == 1),
+                            )
+                nc.scalar.activation(ctx[:, h, :], ctx_ps[:], ACT.Identity, bias=bv_sb[:, h : h + 1], scale=1.0)
+            return ctx
+
+        def project_out(s, ctx):
+            for m in range(CHUNKS):
+                out_ps = psum.tile([P, SEQ_LEN], F32, name="out_ps", tag="proj_ps")
+                for h in range(HEADS):
+                    nc.tensor.matmul(
+                        out_ps[:], wo_sb[:, h, m * P : (m + 1) * P], ctx[:, h, :],
+                        start=(h == 0), stop=(h == HEADS - 1),
+                    )
+                out_sb = work.tile([P, SEQ_LEN], F32, name="out_sb")
+                nc.vector.tensor_scalar_add(out_sb[:], out_ps[:], bo_sb[:, m : m + 1])
+                nc.sync.dma_start(out[m * P : (m + 1) * P, s * SEQ_LEN : (s + 1) * SEQ_LEN], out_sb[:])
+
+        gather(0)
+        query_now = project(0)
+        for s in range(SEQS):
+            if s + 1 < SEQS:
+                gather(s + 1)
+                query_next = project(s + 1)
+            else:
+                query_next = None
+                project_values(value_blocks - 1, 1)
+            project_out(s, attend(s, query_now))
+            query_now = query_next

@@ -17,6 +17,10 @@ PADDED = TOKENS + 2 * REACH
 BLOCKS = SEQ_LEN // P
 SPAN = P + 2 * REACH
 MASKED = -1.0e30
+UNITS_PER_SEQ = HEADS * BLOCKS // 2
+UNITS = SEQS * UNITS_PER_SEQ
+FLIP_LAG = 2
+WEIGH_LAG = 3
 
 BAND_PAIRS = SEQS * (SEQ_LEN * (2 * REACH + 1) - REACH * (REACH + 1))
 FLOPS = 4 * 2 * EMBED * EMBED * TOKENS + 2 * 2 * HEAD_DIM * HEADS * BAND_PAIRS
@@ -38,13 +42,13 @@ def tile_textclassifier_b_kernel(tc, emb, wq, bq, wk, wv, bv, wo, bo, offs, out)
 
         def load_weight(w, name):
             tile = held.tile([P, CHUNKS, EMBED], BF16, name=name)
-            nc.scalar.dma_start(tile[:], w.rearrange("(c p) m -> p c m", p=P))
+            nc.sync.dma_start(tile[:], w.rearrange("(c p) m -> p c m", p=P))
             return tile
 
         def load_bias(b, name):
             tile = held.tile([P, CHUNKS], F32, name=name)
             with nc.allow_non_contiguous_dma(reason="one value to a partition"):
-                nc.scalar.dma_start(tile[:], b.rearrange("(c p) o -> p (c o)", p=P))
+                nc.sync.dma_start(tile[:], b.rearrange("(c p) o -> p (c o)", p=P))
             return tile
 
         wq_sb, wk_sb = load_weight(wq, "wq_sb"), load_weight(wk, "wk_sb")
@@ -54,39 +58,66 @@ def tile_textclassifier_b_kernel(tc, emb, wq, bq, wk, wv, bv, wo, bo, offs, out)
         ident = held.tile([P, P], BF16, name="ident")
         make_identity(nc, ident[:])
 
-        band = [held.tile([P, SPAN], BF16, name=f"band{b}") for b in range(BLOCKS)]
+        band = held.tile([P, BLOCKS, SPAN], BF16, name="band")
+        nc.gpsimd.memset(band[:], 0.0)
         for b in range(BLOCKS):
-            nc.gpsimd.memset(band[b][:], 0.0)
             nc.gpsimd.affine_select(
-                out=band[b][:], in_=band[b][:], pattern=[[1, SPAN]], compare_op=ALU.is_ge,
+                out=band[:, b, :], in_=band[:, b, :], pattern=[[1, SPAN]], compare_op=ALU.is_ge,
                 fill=MASKED, base=0, channel_multiplier=-1,
             )
             nc.gpsimd.affine_select(
-                out=band[b][:], in_=band[b][:], pattern=[[-1, SPAN]], compare_op=ALU.is_ge,
+                out=band[:, b, :], in_=band[:, b, :], pattern=[[-1, SPAN]], compare_op=ALU.is_ge,
                 fill=MASKED, base=2 * REACH, channel_multiplier=1,
             )
-        nc.gpsimd.memset(band[0][:, 0:REACH], MASKED)
-        nc.gpsimd.memset(band[BLOCKS - 1][:, SPAN - REACH : SPAN], MASKED)
+        nc.gpsimd.memset(band[:, 0, 0:REACH], MASKED)
+        nc.gpsimd.memset(band[:, BLOCKS - 1, SPAN - REACH : SPAN], MASKED)
 
         x_pad = held.tile([P, CHUNKS, PADDED], BF16, name="x_pad")
-        keys = held.tile([P, HEADS, PADDED], BF16, name="keys")
-        for padded in (x_pad, keys):
-            nc.gpsimd.memset(padded[:, :, 0:REACH], 0.0)
-            nc.gpsimd.memset(padded[:, :, PADDED - REACH : PADDED], 0.0)
+        nc.gpsimd.memset(x_pad[:, :, 0:REACH], 0.0)
+        nc.gpsimd.memset(x_pad[:, :, PADDED - REACH : PADDED], 0.0)
         value_blocks = PADDED // P
         values = held.tile([P, value_blocks, EMBED], BF16, name="values")
 
-        def gather(s):
+        def gather(s, c):
             piece = offsets[:, s * (SEQ_LEN // 16) : (s + 1) * (SEQ_LEN // 16)]
-            for c in range(CHUNKS):
-                picked = work.tile([P, SEQ_LEN], F32, name="picked")
-                nc.scalar.activation(picked[:], table[c][:].indirect(piece), ACT.Copy)
-                nc.gpsimd.tensor_scalar(
-                    x_pad[:, c, REACH + s * SEQ_LEN : REACH + (s + 1) * SEQ_LEN], picked[:],
-                    1.0, 0.0, op0=ALU.mult, op1=ALU.add,
-                )
+            picked = work.tile([P, SEQ_LEN], F32, name="picked")
+            nc.scalar.activation(picked[:], table[c][:].indirect(piece), ACT.Copy)
+            nc.gpsimd.tensor_scalar(
+                x_pad[:, c, REACH + s * SEQ_LEN : REACH + (s + 1) * SEQ_LEN], picked[:],
+                1.0, 0.0, op0=ALU.mult, op1=ALU.add,
+            )
 
-        def project_values(first, count):
+        def project(weights, m, moving):
+            proj_ps = psum.tile([P, SEQ_LEN], F32, name="proj_ps")
+            for c in range(CHUNKS):
+                nc.tensor.matmul(
+                    proj_ps[:], weights[:, c, m * P : (m + 1) * P], moving[:, c, :],
+                    start=(c == 0), stop=(c == CHUNKS - 1),
+                )
+            return proj_ps
+
+        query, keys = {}, {}
+
+        def x_of(s):
+            return x_pad[:, :, REACH + s * SEQ_LEN : REACH + (s + 1) * SEQ_LEN]
+
+        def project_query(s, h):
+            if h == 0:
+                query[s] = work.tile([P, HEADS, SEQ_LEN], BF16, name="query")
+            nc.vector.tensor_scalar(
+                query[s][:, h, :], project(wq_sb, h, x_of(s))[:], bq_sb[:, h : h + 1], HEAD_DIM ** -0.5,
+                op0=ALU.add, op1=ALU.mult,
+            )
+
+        def project_key(s, h, on_scalar):
+            if h == 0:
+                keys[s] = work.tile([P, HEADS, SEQ_LEN], BF16, name="keys")
+            if on_scalar:
+                nc.scalar.copy(keys[s][:, h, :], project(wk_sb, h, x_of(s))[:])
+            else:
+                nc.vector.tensor_copy(keys[s][:, h, :], project(wk_sb, h, x_of(s))[:])
+
+        def project_values(first, count, on_scalar):
             value_ps = psum.tile([P, 2, EMBED], F32, name="value_ps", tag="proj_ps")
             for k in range(count):
                 g = first + k
@@ -95,106 +126,126 @@ def tile_textclassifier_b_kernel(tc, emb, wq, bq, wk, wv, bv, wo, bo, offs, out)
                         value_ps[:, k, :], x_pad[:, c, g * P : (g + 1) * P], wv_sb[:, c, :],
                         start=(c == 0), stop=(c == CHUNKS - 1),
                     )
-            nc.vector.tensor_copy(values[:, first : first + count, :], value_ps[:, 0:count, :])
-
-        def project(s):
-            lo = REACH + s * SEQ_LEN
-            query = work.tile([P, HEADS, SEQ_LEN], BF16, name="query")
-            for h in range(HEADS):
-                query_ps = psum.tile([P, SEQ_LEN], F32, name="query_ps", tag="proj_ps")
-                for c in range(CHUNKS):
-                    nc.tensor.matmul(
-                        query_ps[:], wq_sb[:, c, h * P : (h + 1) * P], x_pad[:, c, lo : lo + SEQ_LEN],
-                        start=(c == 0), stop=(c == CHUNKS - 1),
-                    )
-                nc.vector.tensor_scalar(
-                    query[:, h, :], query_ps[:], bq_sb[:, h : h + 1], HEAD_DIM ** -0.5,
-                    op0=ALU.add, op1=ALU.mult,
-                )
-                key_ps = psum.tile([P, SEQ_LEN], F32, name="key_ps", tag="proj_ps")
-                for c in range(CHUNKS):
-                    nc.tensor.matmul(
-                        key_ps[:], wk_sb[:, c, h * P : (h + 1) * P], x_pad[:, c, lo : lo + SEQ_LEN],
-                        start=(c == 0), stop=(c == CHUNKS - 1),
-                    )
-                nc.scalar.copy(keys[:, h, lo : lo + SEQ_LEN], key_ps[:])
-            for first in range(BLOCKS * s, BLOCKS * (s + 1), 2):
-                project_values(first, 2)
-            return query
-
-        def attend(s, query):
-            ctx = work.tile([P, HEADS, SEQ_LEN], BF16, name="ctx")
-            for h in range(HEADS):
-                ctx_ps = psum.tile([P, SEQ_LEN], F32, name="ctx_ps")
-                for first in range(0, BLOCKS, 2):
-                    score_ps = psum.tile([P, 2, SPAN], F32, name="score_ps")
-                    for k in range(2):
-                        b = first + k
-                        nc.tensor.matmul(score_ps[:, k, :], ident[:], band[b][:], start=True, stop=False)
-                        nc.tensor.matmul(
-                            score_ps[:, k, :], query[:, h, b * P : (b + 1) * P],
-                            keys[:, h, s * SEQ_LEN + b * P : s * SEQ_LEN + b * P + SPAN],
-                            start=False, stop=True,
-                        )
-                    neg_max = stats.tile([P, 2], F32, name="neg_max")
-                    nc.vector.tensor_reduce(
-                        out=neg_max[:], in_=score_ps[:], axis=mybir.AxisListType.X, op=ALU.max, negate=True
-                    )
-                    expo = work.tile([P, 2, SPAN], F32, name="expo")
-                    total = stats.tile([P, 2], F32, name="total")
-                    for k in range(2):
-                        nc.scalar.activation(
-                            expo[:, k, :], score_ps[:, k, :], ACT.Exp,
-                            bias=neg_max[:, k : k + 1], scale=1.0, accum_out=total[:, k : k + 1],
-                        )
-                    inverse = stats.tile([P, 2], F32, name="inverse")
-                    nc.vector.reciprocal(inverse[:], total[:])
-                    prob = work.tile([P, 2, SPAN], BF16, name="prob")
-                    for k in range(2):
-                        nc.gpsimd.tensor_scalar(
-                            prob[:, k, :], expo[:, k, :], inverse[:, k : k + 1], 0.0,
-                            op0=ALU.mult, op1=ALU.add,
-                        )
-                    prob_t_ps = psum.tile([P, 4, P], BF16, name="prob_t_ps")
-                    for k in range(2):
-                        for half in range(2):
-                            nc.tensor.transpose(
-                                prob_t_ps[:, 2 * k + half, :], prob[:, k, half * P : (half + 1) * P], ident[:]
-                            )
-                    prob_t = work.tile([P, 4, P], BF16, name="prob_t")
-                    nc.vector.tensor_copy(prob_t[:], prob_t_ps[:])
-                    for k in range(2):
-                        b = first + k
-                        for half in range(2):
-                            nc.tensor.matmul(
-                                ctx_ps[:, b * P : (b + 1) * P],
-                                values[:, BLOCKS * s + b + half, h * P : (h + 1) * P],
-                                prob_t[:, 2 * k + half, :],
-                                start=(half == 0), stop=(half == 1),
-                            )
-                nc.scalar.activation(ctx[:, h, :], ctx_ps[:], ACT.Identity, bias=bv_sb[:, h : h + 1], scale=1.0)
-            return ctx
-
-        def project_out(s, ctx):
-            for m in range(CHUNKS):
-                out_ps = psum.tile([P, SEQ_LEN], F32, name="out_ps", tag="proj_ps")
-                for h in range(HEADS):
-                    nc.tensor.matmul(
-                        out_ps[:], wo_sb[:, h, m * P : (m + 1) * P], ctx[:, h, :],
-                        start=(h == 0), stop=(h == HEADS - 1),
-                    )
-                out_sb = work.tile([P, SEQ_LEN], F32, name="out_sb")
-                nc.vector.tensor_scalar_add(out_sb[:], out_ps[:], bo_sb[:, m : m + 1])
-                nc.sync.dma_start(out[m * P : (m + 1) * P, s * SEQ_LEN : (s + 1) * SEQ_LEN], out_sb[:])
-
-        gather(0)
-        query_now = project(0)
-        for s in range(SEQS):
-            if s + 1 < SEQS:
-                gather(s + 1)
-                query_next = project(s + 1)
+            if on_scalar:
+                nc.scalar.copy(values[:, first : first + count, :], value_ps[:, 0:count, :])
             else:
-                query_next = None
-                project_values(value_blocks - 1, 1)
-            project_out(s, attend(s, query_now))
-            query_now = query_next
+                nc.vector.tensor_copy(values[:, first : first + count, :], value_ps[:, 0:count, :])
+
+        def place(u):
+            return u // UNITS_PER_SEQ, (u % UNITS_PER_SEQ) // 2, 2 * (u % 2)
+
+        expo, total = {}, {}
+        prob, prob_t = {}, {}
+        ctx_ps, ctx = {}, {}
+
+        def exponentials(u):
+            s, h, first = place(u)
+            score_ps = psum.tile([P, 2, SPAN], F32, name="score_ps")
+            nc.tensor.matmul(score_ps[:], ident[:], band[:, first : first + 2, :], start=True, stop=False)
+            for k in range(2):
+                b = first + k
+                origin = b * P - REACH
+                near, far = max(-origin, 0), min(SEQ_LEN - origin, SPAN)
+                nc.tensor.matmul(
+                    score_ps[:, k, near:far], query[s][:, h, b * P : (b + 1) * P],
+                    keys[s][:, h, origin + near : origin + far], start=False, stop=(k == 1),
+                )
+            neg_max = stats.tile([P, 2], F32, name="neg_max")
+            nc.vector.tensor_reduce(
+                out=neg_max[:], in_=score_ps[:], axis=mybir.AxisListType.X, op=ALU.max, negate=True
+            )
+            expo[u] = work.tile([P, 2, SPAN], F32, name="expo")
+            total[u] = stats.tile([P, 2], F32, name="total")
+            for k in range(2):
+                nc.scalar.activation(
+                    expo[u][:, k, :], score_ps[:, k, :], ACT.Exp,
+                    bias=neg_max[:, k : k + 1], scale=1.0, accum_out=total[u][:, k : k + 1],
+                )
+
+        def normalise(u):
+            inverse = stats.tile([P, 2], F32, name="inverse")
+            nc.vector.reciprocal(inverse[:], total[u][:])
+            prob[u] = work.tile([P, 2, SPAN], BF16, name="prob")
+            for k in range(2):
+                nc.gpsimd.tensor_scalar(
+                    prob[u][:, k, :], expo[u][:, k, :], inverse[:, k : k + 1], 0.0,
+                    op0=ALU.mult, op1=ALU.add,
+                )
+
+        def flip(u):
+            prob_t_ps = psum.tile([P, 4, P], BF16, name="prob_t_ps")
+            for k in range(2):
+                for half in range(2):
+                    nc.tensor.transpose(
+                        prob_t_ps[:, 2 * k + half, :], prob[u][:, k, half * P : (half + 1) * P], ident[:]
+                    )
+            prob_t[u] = work.tile([P, 4, P], BF16, name="prob_t")
+            nc.vector.tensor_copy(prob_t[u][:], prob_t_ps[:])
+
+        def weigh(u):
+            s, h, first = place(u)
+            if first == 0:
+                ctx_ps[s, h] = psum.tile([P, SEQ_LEN], F32, name="ctx_ps")
+            g = BLOCKS * s + first
+            nc.tensor.matmul(
+                ctx_ps[s, h][:, first * P : (first + 2) * P], values[:, g + 1, h * P : (h + 1) * P],
+                prob_t[u][:, 1:3, :], start=True, stop=False,
+            )
+            nc.tensor.matmul(
+                ctx_ps[s, h][:, first * P : (first + 1) * P], values[:, g, h * P : (h + 1) * P],
+                prob_t[u][:, 0, :], start=False, stop=False,
+            )
+            nc.tensor.matmul(
+                ctx_ps[s, h][:, (first + 1) * P : (first + 2) * P], values[:, g + 2, h * P : (h + 1) * P],
+                prob_t[u][:, 3, :], start=False, stop=True,
+            )
+            if first + 2 == BLOCKS:
+                if h == 0:
+                    ctx[s] = work.tile([P, HEADS, SEQ_LEN], BF16, name="ctx")
+                nc.scalar.activation(
+                    ctx[s][:, h, :], ctx_ps[s, h][:], ACT.Identity, bias=bv_sb[:, h : h + 1], scale=1.0
+                )
+
+        def project_out(s, m):
+            out_sb = work.tile([P, SEQ_LEN], F32, name="out_sb")
+            nc.vector.tensor_scalar_add(out_sb[:], project(wo_sb, m, ctx[s])[:], bo_sb[:, m : m + 1])
+            nc.sync.dma_start(out[m * P : (m + 1) * P, s * SEQ_LEN : (s + 1) * SEQ_LEN], out_sb[:])
+
+        def side_work(s, quarter, part):
+            if quarter < 2 and s + 1 < SEQS:
+                if part == 0:
+                    project_query(s + 1, quarter)
+                else:
+                    project_key(s + 1, quarter, on_scalar=(quarter % 2 == 0))
+            if quarter == 2 and s + 1 < SEQS:
+                project_values(BLOCKS * (s + 1) + 2 * part, 2, on_scalar=(part == 1))
+            if quarter == 2 and s + 1 == SEQS and part == 0:
+                project_values(value_blocks - 1, 1, on_scalar=False)
+            if quarter == 3 and s >= 1:
+                project_out(s - 1, part)
+
+        for c in range(CHUNKS):
+            for s in range(2):
+                gather(s, c)
+        for h in range(HEADS):
+            project_query(0, h)
+            project_key(0, h, on_scalar=True)
+        for first in range(0, BLOCKS, 2):
+            project_values(first, 2, on_scalar=False)
+
+        for u in range(UNITS + WEIGH_LAG):
+            s, quarter = u // UNITS_PER_SEQ, u % UNITS_PER_SEQ
+            if u < UNITS:
+                if quarter % 2 == 1 and s + 2 < SEQS:
+                    gather(s + 2, quarter // 2)
+                exponentials(u)
+            if FLIP_LAG <= u < UNITS + FLIP_LAG:
+                flip(u - FLIP_LAG)
+            if u < UNITS:
+                side_work(s, quarter, 0)
+                normalise(u)
+                side_work(s, quarter, 1)
+            if u >= WEIGH_LAG:
+                weigh(u - WEIGH_LAG)
+        for m in range(CHUNKS):
+            project_out(SEQS - 1, m)

@@ -21,6 +21,7 @@ UNITS_PER_SEQ = HEADS * BLOCKS // 2
 UNITS = SEQS * UNITS_PER_SEQ
 FLIP_LAG = 2
 WEIGH_LAG = 3
+OUT_LAG = UNITS_PER_SEQ + WEIGH_LAG
 
 BAND_PAIRS = SEQS * (SEQ_LEN * (2 * REACH + 1) - REACH * (REACH + 1))
 FLOPS = 4 * 2 * EMBED * EMBED * TOKENS + 2 * 2 * HEAD_DIM * HEADS * BAND_PAIRS
@@ -88,7 +89,7 @@ def tile_textclassifier_b_kernel(tc, emb, wq, bq, wk, wv, bv, wo, bo, offs, out)
             )
 
         def project(weights, m, moving):
-            proj_ps = psum.tile([P, SEQ_LEN], F32, name="proj_ps")
+            proj_ps = psum.tile([P, SEQ_LEN], F32, name="proj_ps", bufs=3)
             for c in range(CHUNKS):
                 nc.tensor.matmul(
                     proj_ps[:], weights[:, c, m * P : (m + 1) * P], moving[:, c, :],
@@ -118,7 +119,7 @@ def tile_textclassifier_b_kernel(tc, emb, wq, bq, wk, wv, bv, wo, bo, offs, out)
                 nc.vector.tensor_copy(keys[s][:, h, :], project(wk_sb, h, x_of(s))[:])
 
         def project_values(first, count, on_scalar):
-            value_ps = psum.tile([P, 2, EMBED], F32, name="value_ps", tag="proj_ps")
+            value_ps = psum.tile([P, 2, EMBED], F32, name="value_ps", tag="proj_ps", bufs=3)
             for k in range(count):
                 g = first + k
                 for c in range(CHUNKS):
@@ -135,8 +136,16 @@ def tile_textclassifier_b_kernel(tc, emb, wq, bq, wk, wv, bv, wo, bo, offs, out)
             return u // UNITS_PER_SEQ, (u % UNITS_PER_SEQ) // 2, 2 * (u % 2)
 
         expo, total = {}, {}
-        prob, prob_t = {}, {}
-        ctx_ps, ctx = {}, {}
+        prob_t = {}
+
+        def inside(b):
+            return max(REACH - b * P, 0), min(SEQ_LEN + REACH - b * P, SPAN)
+
+        prob = [held.tile([P, 2, SPAN], BF16, name=f"prob{i}") for i in range(4)]
+        for i in range(4):
+            nc.gpsimd.memset(prob[i][:], 0.0)
+        ctx_ps = {}
+        ctx = held.tile([P, HEADS, TOKENS], BF16, name="ctx")
 
         def exponentials(u):
             s, h, first = place(u)
@@ -144,11 +153,10 @@ def tile_textclassifier_b_kernel(tc, emb, wq, bq, wk, wv, bv, wo, bo, offs, out)
             nc.tensor.matmul(score_ps[:], ident[:], band[:, first : first + 2, :], start=True, stop=False)
             for k in range(2):
                 b = first + k
-                origin = b * P - REACH
-                near, far = max(-origin, 0), min(SEQ_LEN - origin, SPAN)
+                near, far = inside(b)
                 nc.tensor.matmul(
                     score_ps[:, k, near:far], query[s][:, h, b * P : (b + 1) * P],
-                    keys[s][:, h, origin + near : origin + far], start=False, stop=(k == 1),
+                    keys[s][:, h, b * P - REACH + near : b * P - REACH + far], start=False, stop=(k == 1),
                 )
             neg_max = stats.tile([P, 2], F32, name="neg_max")
             nc.vector.tensor_reduce(
@@ -157,27 +165,28 @@ def tile_textclassifier_b_kernel(tc, emb, wq, bq, wk, wv, bv, wo, bo, offs, out)
             expo[u] = work.tile([P, 2, SPAN], F32, name="expo")
             total[u] = stats.tile([P, 2], F32, name="total")
             for k in range(2):
+                near, far = inside(first + k)
                 nc.scalar.activation(
-                    expo[u][:, k, :], score_ps[:, k, :], ACT.Exp,
+                    expo[u][:, k, near:far], score_ps[:, k, near:far], ACT.Exp,
                     bias=neg_max[:, k : k + 1], scale=1.0, accum_out=total[u][:, k : k + 1],
                 )
 
         def normalise(u):
             inverse = stats.tile([P, 2], F32, name="inverse")
             nc.vector.reciprocal(inverse[:], total[u][:])
-            prob[u] = work.tile([P, 2, SPAN], BF16, name="prob")
             for k in range(2):
+                near, far = inside(place(u)[2] + k)
                 nc.gpsimd.tensor_scalar(
-                    prob[u][:, k, :], expo[u][:, k, :], inverse[:, k : k + 1], 0.0,
+                    prob[u % 4][:, k, near:far], expo[u][:, k, near:far], inverse[:, k : k + 1], 0.0,
                     op0=ALU.mult, op1=ALU.add,
                 )
 
         def flip(u):
-            prob_t_ps = psum.tile([P, 4, P], BF16, name="prob_t_ps")
+            prob_t_ps = psum.tile([P, 4, P], BF16, name="prob_t_ps", bufs=1)
             for k in range(2):
                 for half in range(2):
                     nc.tensor.transpose(
-                        prob_t_ps[:, 2 * k + half, :], prob[u][:, k, half * P : (half + 1) * P], ident[:]
+                        prob_t_ps[:, 2 * k + half, :], prob[u % 4][:, k, half * P : (half + 1) * P], ident[:]
                     )
             prob_t[u] = work.tile([P, 4, P], BF16, name="prob_t")
             nc.vector.tensor_copy(prob_t[u][:], prob_t_ps[:])
@@ -200,29 +209,38 @@ def tile_textclassifier_b_kernel(tc, emb, wq, bq, wk, wv, bv, wo, bo, offs, out)
                 prob_t[u][:, 3, :], start=False, stop=True,
             )
             if first + 2 == BLOCKS:
-                if h == 0:
-                    ctx[s] = work.tile([P, HEADS, SEQ_LEN], BF16, name="ctx")
                 nc.scalar.activation(
-                    ctx[s][:, h, :], ctx_ps[s, h][:], ACT.Identity, bias=bv_sb[:, h : h + 1], scale=1.0
+                    ctx[:, h, s * SEQ_LEN : (s + 1) * SEQ_LEN], ctx_ps[s, h][:], ACT.Identity,
+                    bias=bv_sb[:, h : h + 1], scale=1.0,
                 )
 
-        def project_out(s, m):
+        def project_out(s, m, on_scalar):
+            out_ps = project(wo_sb, m, ctx[:, :, s * SEQ_LEN : (s + 1) * SEQ_LEN])
             out_sb = work.tile([P, SEQ_LEN], F32, name="out_sb")
-            nc.vector.tensor_scalar_add(out_sb[:], project(wo_sb, m, ctx[s])[:], bo_sb[:, m : m + 1])
+            if on_scalar:
+                nc.scalar.activation(out_sb[:], out_ps[:], ACT.Identity, bias=bo_sb[:, m : m + 1], scale=1.0)
+            else:
+                nc.vector.tensor_scalar_add(out_sb[:], out_ps[:], bo_sb[:, m : m + 1])
             nc.sync.dma_start(out[m * P : (m + 1) * P, s * SEQ_LEN : (s + 1) * SEQ_LEN], out_sb[:])
 
+        def looks_up(s, quarter):
+            return quarter % 2 == 1 and s + 2 < SEQS
+
         def side_work(s, quarter, part):
+            on_scalar = part == 1 and not looks_up(s, quarter)
             if quarter < 2 and s + 1 < SEQS:
                 if part == 0:
                     project_query(s + 1, quarter)
                 else:
-                    project_key(s + 1, quarter, on_scalar=(quarter % 2 == 0))
+                    project_key(s + 1, quarter, on_scalar)
             if quarter == 2 and s + 1 < SEQS:
-                project_values(BLOCKS * (s + 1) + 2 * part, 2, on_scalar=(part == 1))
+                project_values(BLOCKS * (s + 1) + 2 * part, 2, on_scalar)
             if quarter == 2 and s + 1 == SEQS and part == 0:
-                project_values(value_blocks - 1, 1, on_scalar=False)
-            if quarter == 3 and s >= 1:
-                project_out(s - 1, part)
+                project_values(value_blocks - 1, 1, on_scalar)
+            if quarter == 3 and OUT_LAG <= s < SEQS - 1:
+                project_out(s - OUT_LAG, part, on_scalar)
+            if s >= SEQS - 1:
+                project_out(UNITS_PER_SEQ * s + quarter - (UNITS - UNITS_PER_SEQ) + SEQS - 1 - OUT_LAG, part, on_scalar)
 
         for c in range(CHUNKS):
             for s in range(2):
@@ -231,21 +249,21 @@ def tile_textclassifier_b_kernel(tc, emb, wq, bq, wk, wv, bv, wo, bo, offs, out)
             project_query(0, h)
             project_key(0, h, on_scalar=True)
         for first in range(0, BLOCKS, 2):
-            project_values(first, 2, on_scalar=False)
+            project_values(first, 2, on_scalar=(first > 0))
 
         for u in range(UNITS + WEIGH_LAG):
             s, quarter = u // UNITS_PER_SEQ, u % UNITS_PER_SEQ
             if u < UNITS:
-                if quarter % 2 == 1 and s + 2 < SEQS:
+                if looks_up(s, quarter):
                     gather(s + 2, quarter // 2)
                 exponentials(u)
             if FLIP_LAG <= u < UNITS + FLIP_LAG:
                 flip(u - FLIP_LAG)
+            side_work(s, quarter, 0)
             if u < UNITS:
-                side_work(s, quarter, 0)
                 normalise(u)
-                side_work(s, quarter, 1)
+            side_work(s, quarter, 1)
             if u >= WEIGH_LAG:
                 weigh(u - WEIGH_LAG)
         for m in range(CHUNKS):
-            project_out(SEQS - 1, m)
+            project_out(SEQS - 1, m, on_scalar=(m > 0))

@@ -17,11 +17,17 @@ PADDED = TOKENS + 2 * REACH
 BLOCKS = SEQ_LEN // P
 SPAN = P + 2 * REACH
 MASKED = -1.0e30
-UNITS_PER_SEQ = HEADS * BLOCKS // 2
+
+PAIR = 2
+UNITS_PER_SEQ = HEADS * BLOCKS // PAIR
 UNITS = SEQS * UNITS_PER_SEQ
+LAST_SEQ_START = UNITS - UNITS_PER_SEQ
 FLIP_LAG = 2
 WEIGH_LAG = 3
+LOOK_AHEAD = 2
+PROB_RING = FLIP_LAG + 2
 OUT_LAG = UNITS_PER_SEQ + WEIGH_LAG
+BEFORE_ATTENTION = 2 * HEADS + BLOCKS // PAIR
 
 BAND_PAIRS = SEQS * (SEQ_LEN * (2 * REACH + 1) - REACH * (REACH + 1))
 FLOPS = 4 * 2 * EMBED * EMBED * TOKENS + 2 * 2 * HEAD_DIM * HEADS * BAND_PAIRS
@@ -42,15 +48,15 @@ def tile_textclassifier_b_kernel(tc, emb, wq, bq, wk, wv, bv, wo, bo, offs, out)
             nc.sync.dma_start(table[c][:], emb[c * P : (c + 1) * P, :])
 
         def load_weight(w, name):
-            tile = held.tile([P, CHUNKS, EMBED], BF16, name=name)
-            nc.sync.dma_start(tile[:], w.rearrange("(c p) m -> p c m", p=P))
-            return tile
+            loaded = held.tile([P, CHUNKS, EMBED], BF16, name=name)
+            nc.sync.dma_start(loaded[:], w.rearrange("(c p) m -> p c m", p=P))
+            return loaded
 
-        def load_bias(b, name):
-            tile = held.tile([P, CHUNKS], F32, name=name)
+        def load_bias(bias, name):
+            loaded = held.tile([P, CHUNKS], F32, name=name)
             with nc.allow_non_contiguous_dma(reason="one value to a partition"):
-                nc.sync.dma_start(tile[:], b.rearrange("(c p) o -> p (c o)", p=P))
-            return tile
+                nc.sync.dma_start(loaded[:], bias.rearrange("(c p) o -> p (c o)", p=P))
+            return loaded
 
         wq_sb, wk_sb = load_weight(wq, "wq_sb"), load_weight(wk, "wk_sb")
         wv_sb, wo_sb = load_weight(wv, "wv_sb"), load_weight(wo, "wo_sb")
@@ -73,20 +79,29 @@ def tile_textclassifier_b_kernel(tc, emb, wq, bq, wk, wv, bv, wo, bo, offs, out)
         nc.gpsimd.memset(band[:, 0, 0:REACH], MASKED)
         nc.gpsimd.memset(band[:, BLOCKS - 1, SPAN - REACH : SPAN], MASKED)
 
+        def inside(b):
+            return max(REACH - b * P, 0), min(SEQ_LEN + REACH - b * P, SPAN)
+
         x_pad = held.tile([P, CHUNKS, PADDED], BF16, name="x_pad")
         nc.gpsimd.memset(x_pad[:, :, 0:REACH], 0.0)
         nc.gpsimd.memset(x_pad[:, :, PADDED - REACH : PADDED], 0.0)
         value_blocks = PADDED // P
         values = held.tile([P, value_blocks, EMBED], BF16, name="values")
+        ctx = held.tile([P, HEADS, TOKENS], BF16, name="ctx")
+        prob = [held.tile([P, PAIR, SPAN], BF16, name=f"prob{slot}") for slot in range(PROB_RING)]
+        for slot in range(PROB_RING):
+            nc.gpsimd.memset(prob[slot][:], 0.0)
+
+        query, keys = {}, {}
+        expo, total = {}, {}
+        prob_t = {}
+        ctx_ps = {}
 
         def gather(s, c):
             piece = offsets[:, s * (SEQ_LEN // 16) : (s + 1) * (SEQ_LEN // 16)]
             picked = work.tile([P, SEQ_LEN], F32, name="picked")
             nc.scalar.activation(picked[:], table[c][:].indirect(piece), ACT.Copy)
-            nc.gpsimd.tensor_scalar(
-                x_pad[:, c, REACH + s * SEQ_LEN : REACH + (s + 1) * SEQ_LEN], picked[:],
-                1.0, 0.0, op0=ALU.mult, op1=ALU.add,
-            )
+            nc.vector.tensor_copy(x_pad[:, c, REACH + s * SEQ_LEN : REACH + (s + 1) * SEQ_LEN], picked[:])
 
         def project(weights, m, moving):
             proj_ps = psum.tile([P, SEQ_LEN], F32, name="proj_ps", bufs=3)
@@ -96,8 +111,6 @@ def tile_textclassifier_b_kernel(tc, emb, wq, bq, wk, wv, bv, wo, bo, offs, out)
                     start=(c == 0), stop=(c == CHUNKS - 1),
                 )
             return proj_ps
-
-        query, keys = {}, {}
 
         def x_of(s):
             return x_pad[:, :, REACH + s * SEQ_LEN : REACH + (s + 1) * SEQ_LEN]
@@ -118,53 +131,49 @@ def tile_textclassifier_b_kernel(tc, emb, wq, bq, wk, wv, bv, wo, bo, offs, out)
             else:
                 nc.vector.tensor_copy(keys[s][:, h, :], project(wk_sb, h, x_of(s))[:])
 
-        def project_values(first, count, on_scalar):
-            value_ps = psum.tile([P, 2, EMBED], F32, name="value_ps", tag="proj_ps", bufs=3)
+        def project_values(g, count, on_scalar):
+            value_ps = psum.tile([P, PAIR, EMBED], F32, name="value_ps", tag="proj_ps", bufs=3)
             for k in range(count):
-                g = first + k
                 for c in range(CHUNKS):
                     nc.tensor.matmul(
-                        value_ps[:, k, :], x_pad[:, c, g * P : (g + 1) * P], wv_sb[:, c, :],
+                        value_ps[:, k, :], x_pad[:, c, (g + k) * P : (g + k + 1) * P], wv_sb[:, c, :],
                         start=(c == 0), stop=(c == CHUNKS - 1),
                     )
             if on_scalar:
-                nc.scalar.copy(values[:, first : first + count, :], value_ps[:, 0:count, :])
+                nc.scalar.copy(values[:, g : g + count, :], value_ps[:, 0:count, :])
             else:
-                nc.vector.tensor_copy(values[:, first : first + count, :], value_ps[:, 0:count, :])
+                nc.vector.tensor_copy(values[:, g : g + count, :], value_ps[:, 0:count, :])
+
+        def project_out(s, m, on_scalar):
+            out_ps = project(wo_sb, m, ctx[:, :, s * SEQ_LEN : (s + 1) * SEQ_LEN])
+            out_sb = work.tile([P, SEQ_LEN], F32, name="out_sb")
+            if on_scalar:
+                nc.scalar.activation(out_sb[:], out_ps[:], ACT.Identity, bias=bo_sb[:, m : m + 1], scale=1.0)
+            else:
+                nc.vector.tensor_scalar_add(out_sb[:], out_ps[:], bo_sb[:, m : m + 1])
+            nc.sync.dma_start(out[m * P : (m + 1) * P, s * SEQ_LEN : (s + 1) * SEQ_LEN], out_sb[:])
 
         def place(u):
-            return u // UNITS_PER_SEQ, (u % UNITS_PER_SEQ) // 2, 2 * (u % 2)
-
-        expo, total = {}, {}
-        prob_t = {}
-
-        def inside(b):
-            return max(REACH - b * P, 0), min(SEQ_LEN + REACH - b * P, SPAN)
-
-        prob = [held.tile([P, 2, SPAN], BF16, name=f"prob{i}") for i in range(4)]
-        for i in range(4):
-            nc.gpsimd.memset(prob[i][:], 0.0)
-        ctx_ps = {}
-        ctx = held.tile([P, HEADS, TOKENS], BF16, name="ctx")
+            return u // UNITS_PER_SEQ, (u % UNITS_PER_SEQ) // 2, PAIR * (u % 2)
 
         def exponentials(u):
             s, h, first = place(u)
-            score_ps = psum.tile([P, 2, SPAN], F32, name="score_ps")
-            nc.tensor.matmul(score_ps[:], ident[:], band[:, first : first + 2, :], start=True, stop=False)
-            for k in range(2):
+            score_ps = psum.tile([P, PAIR, SPAN], F32, name="score_ps")
+            nc.tensor.matmul(score_ps[:], ident[:], band[:, first : first + PAIR, :], start=True, stop=False)
+            for k in range(PAIR):
                 b = first + k
                 near, far = inside(b)
                 nc.tensor.matmul(
                     score_ps[:, k, near:far], query[s][:, h, b * P : (b + 1) * P],
-                    keys[s][:, h, b * P - REACH + near : b * P - REACH + far], start=False, stop=(k == 1),
+                    keys[s][:, h, b * P - REACH + near : b * P - REACH + far], start=False, stop=(k == PAIR - 1),
                 )
-            neg_max = stats.tile([P, 2], F32, name="neg_max")
+            neg_max = stats.tile([P, PAIR], F32, name="neg_max")
             nc.vector.tensor_reduce(
                 out=neg_max[:], in_=score_ps[:], axis=mybir.AxisListType.X, op=ALU.max, negate=True
             )
-            expo[u] = work.tile([P, 2, SPAN], F32, name="expo")
-            total[u] = stats.tile([P, 2], F32, name="total")
-            for k in range(2):
+            expo[u] = work.tile([P, PAIR, SPAN], F32, name="expo")
+            total[u] = stats.tile([P, PAIR], F32, name="total")
+            for k in range(PAIR):
                 near, far = inside(first + k)
                 nc.scalar.activation(
                     expo[u][:, k, near:far], score_ps[:, k, near:far], ACT.Exp,
@@ -172,23 +181,25 @@ def tile_textclassifier_b_kernel(tc, emb, wq, bq, wk, wv, bv, wo, bo, offs, out)
                 )
 
         def normalise(u):
-            inverse = stats.tile([P, 2], F32, name="inverse")
+            first = place(u)[2]
+            inverse = stats.tile([P, PAIR], F32, name="inverse")
             nc.vector.reciprocal(inverse[:], total[u][:])
-            for k in range(2):
-                near, far = inside(place(u)[2] + k)
+            for k in range(PAIR):
+                near, far = inside(first + k)
                 nc.gpsimd.tensor_scalar(
-                    prob[u % 4][:, k, near:far], expo[u][:, k, near:far], inverse[:, k : k + 1], 0.0,
+                    prob[u % PROB_RING][:, k, near:far], expo[u][:, k, near:far], inverse[:, k : k + 1], 0.0,
                     op0=ALU.mult, op1=ALU.add,
                 )
 
         def flip(u):
-            prob_t_ps = psum.tile([P, 4, P], BF16, name="prob_t_ps", bufs=1)
-            for k in range(2):
+            prob_t_ps = psum.tile([P, 2 * PAIR, P], BF16, name="prob_t_ps", bufs=1)
+            for k in range(PAIR):
                 for half in range(2):
                     nc.tensor.transpose(
-                        prob_t_ps[:, 2 * k + half, :], prob[u % 4][:, k, half * P : (half + 1) * P], ident[:]
+                        prob_t_ps[:, 2 * k + half, :], prob[u % PROB_RING][:, k, half * P : (half + 1) * P],
+                        ident[:],
                     )
-            prob_t[u] = work.tile([P, 4, P], BF16, name="prob_t")
+            prob_t[u] = work.tile([P, 2 * PAIR, P], BF16, name="prob_t")
             nc.vector.tensor_copy(prob_t[u][:], prob_t_ps[:])
 
         def weigh(u):
@@ -208,62 +219,55 @@ def tile_textclassifier_b_kernel(tc, emb, wq, bq, wk, wv, bv, wo, bo, offs, out)
                 ctx_ps[s, h][:, (first + 1) * P : (first + 2) * P], values[:, g + 2, h * P : (h + 1) * P],
                 prob_t[u][:, 3, :], start=False, stop=True,
             )
-            if first + 2 == BLOCKS:
+            if first + PAIR == BLOCKS:
                 nc.scalar.activation(
                     ctx[:, h, s * SEQ_LEN : (s + 1) * SEQ_LEN], ctx_ps[s, h][:], ACT.Identity,
                     bias=bv_sb[:, h : h + 1], scale=1.0,
                 )
 
-        def project_out(s, m, on_scalar):
-            out_ps = project(wo_sb, m, ctx[:, :, s * SEQ_LEN : (s + 1) * SEQ_LEN])
-            out_sb = work.tile([P, SEQ_LEN], F32, name="out_sb")
-            if on_scalar:
-                nc.scalar.activation(out_sb[:], out_ps[:], ACT.Identity, bias=bo_sb[:, m : m + 1], scale=1.0)
+        def looks_up(u):
+            return u % 2 == 1 and u // UNITS_PER_SEQ + LOOK_AHEAD < SEQS
+
+        def product_before_attention(s, n, on_scalar):
+            if n >= 2 * HEADS:
+                project_values(BLOCKS * s + PAIR * (n - 2 * HEADS), PAIR, on_scalar)
+            elif n % 2 == 0:
+                project_query(s, n // 2)
             else:
-                nc.vector.tensor_scalar_add(out_sb[:], out_ps[:], bo_sb[:, m : m + 1])
-            nc.sync.dma_start(out[m * P : (m + 1) * P, s * SEQ_LEN : (s + 1) * SEQ_LEN], out_sb[:])
+                project_key(s, n // 2, on_scalar)
 
-        def looks_up(s, quarter):
-            return quarter % 2 == 1 and s + 2 < SEQS
-
-        def side_work(s, quarter, part):
-            on_scalar = part == 1 and not looks_up(s, quarter)
-            if quarter < 2 and s + 1 < SEQS:
-                if part == 0:
-                    project_query(s + 1, quarter)
-                else:
-                    project_key(s + 1, quarter, on_scalar)
-            if quarter == 2 and s + 1 < SEQS:
-                project_values(BLOCKS * (s + 1) + 2 * part, 2, on_scalar)
-            if quarter == 2 and s + 1 == SEQS and part == 0:
-                project_values(value_blocks - 1, 1, on_scalar)
-            if quarter == 3 and OUT_LAG <= s < SEQS - 1:
-                project_out(s - OUT_LAG, part, on_scalar)
-            if s >= SEQS - 1:
-                project_out(UNITS_PER_SEQ * s + quarter - (UNITS - UNITS_PER_SEQ) + SEQS - 1 - OUT_LAG, part, on_scalar)
+        def side_product(u, part):
+            s, quarter = divmod(u, UNITS_PER_SEQ)
+            on_scalar = part == 1 and not looks_up(u)
+            if u >= LAST_SEQ_START:
+                if u == LAST_SEQ_START and part == 0:
+                    project_values(value_blocks - 1, 1, on_scalar)
+                project_out(SEQS - 1 - OUT_LAG + u - LAST_SEQ_START, part, on_scalar)
+            elif quarter % 2 == 0:
+                product_before_attention(s + 1, BEFORE_ATTENTION // 2 * (quarter // 2) + part, on_scalar)
+            elif part == 0:
+                product_before_attention(s + 1, BEFORE_ATTENTION // 2 * (quarter // 2) + 2, on_scalar)
+            elif s >= OUT_LAG:
+                project_out(s - OUT_LAG, quarter // 2, on_scalar)
 
         for c in range(CHUNKS):
-            for s in range(2):
+            for s in range(LOOK_AHEAD):
                 gather(s, c)
-        for h in range(HEADS):
-            project_query(0, h)
-            project_key(0, h, on_scalar=True)
-        for first in range(0, BLOCKS, 2):
-            project_values(first, 2, on_scalar=(first > 0))
+        for n in range(BEFORE_ATTENTION):
+            product_before_attention(0, n, on_scalar=(n % 2 == 1))
 
         for u in range(UNITS + WEIGH_LAG):
-            s, quarter = u // UNITS_PER_SEQ, u % UNITS_PER_SEQ
             if u < UNITS:
-                if looks_up(s, quarter):
-                    gather(s + 2, quarter // 2)
+                if looks_up(u):
+                    gather(u // UNITS_PER_SEQ + LOOK_AHEAD, (u % UNITS_PER_SEQ) // 2)
                 exponentials(u)
             if FLIP_LAG <= u < UNITS + FLIP_LAG:
                 flip(u - FLIP_LAG)
-            side_work(s, quarter, 0)
+            side_product(u, 0)
             if u < UNITS:
                 normalise(u)
-            side_work(s, quarter, 1)
+            side_product(u, 1)
             if u >= WEIGH_LAG:
                 weigh(u - WEIGH_LAG)
         for m in range(CHUNKS):
-            project_out(SEQS - 1, m, on_scalar=(m > 0))
+            project_out(SEQS - 1, m, on_scalar=(m == 1))

import concourse.mybir as mybir
from concourse.masks import make_identity

F32, BF16, U16 = mybir.dt.float32, mybir.dt.bfloat16, mybir.dt.uint16
ACT = mybir.ActivationFunctionType
ALU = mybir.AluOpType

P = 128
VOCAB = 4096
EMBED = 256
CHUNKS = EMBED // P
HEADS, HEAD_DIM = 2, 128
SEQS, SEQ_LEN = 12, 512
REACH = 64
TOKENS = SEQS * SEQ_LEN
PADDED = TOKENS + 2 * REACH
BLOCKS = SEQ_LEN // P
SPAN = P + 2 * REACH
MASKED = -1.0e30

PAIR = 2
UNITS_PER_SEQ = HEADS * BLOCKS // PAIR
UNITS = SEQS * UNITS_PER_SEQ
LAST_SEQ_START = UNITS - UNITS_PER_SEQ
FLIP_LAG = 2
WEIGH_LAG = 3
LOOK_AHEAD = 2
PROB_RING = FLIP_LAG + 2
OUT_LAG = UNITS_PER_SEQ + WEIGH_LAG
BEFORE_ATTENTION = 2 * HEADS + BLOCKS // PAIR

BAND_PAIRS = SEQS * (SEQ_LEN * (2 * REACH + 1) - REACH * (REACH + 1))
FLOPS = 4 * 2 * EMBED * EMBED * TOKENS + 2 * 2 * HEAD_DIM * HEADS * BAND_PAIRS


def tile_textclassifier_b_kernel(tc, emb, wq, bq, wk, wv, bv, wo, bo, offs, out):
    nc = tc.nc
    with (
        tc.tile_pool(name="held", bufs=1) as held,
        tc.tile_pool(name="work", bufs=4) as work,
        tc.tile_pool(name="stats", bufs=8) as stats,
        tc.psum_pool(name="psum", bufs=2) as psum,
    ):
        offsets = held.tile([P, TOKENS // 16], U16, name="offsets")
        nc.sync.dma_start(offsets[:], offs)
        table = [held.tile([P, VOCAB], F32, name=f"table{c}") for c in range(CHUNKS)]
        for c in range(CHUNKS):
            nc.sync.dma_start(table[c][:], emb[c * P : (c + 1) * P, :])

        def load_weight(w, name):
            loaded = held.tile([P, CHUNKS, EMBED], BF16, name=name)
            nc.sync.dma_start(loaded[:], w.rearrange("(c p) m -> p c m", p=P))
            return loaded

        def load_bias(bias, name):
            loaded = held.tile([P, CHUNKS], F32, name=name)
            with nc.allow_non_contiguous_dma(reason="one value to a partition"):
                nc.sync.dma_start(loaded[:], bias.rearrange("(c p) o -> p (c o)", p=P))
            return loaded

        wq_sb, wk_sb = load_weight(wq, "wq_sb"), load_weight(wk, "wk_sb")
        wv_sb, wo_sb = load_weight(wv, "wv_sb"), load_weight(wo, "wo_sb")
        bq_sb, bv_sb, bo_sb = load_bias(bq, "bq_sb"), load_bias(bv, "bv_sb"), load_bias(bo, "bo_sb")

        ident = held.tile([P, P], BF16, name="ident")
        make_identity(nc, ident[:])

        band = held.tile([P, BLOCKS, SPAN], BF16, name="band")
        nc.gpsimd.memset(band[:], 0.0)
        for b in range(BLOCKS):
            nc.gpsimd.affine_select(
                out=band[:, b, :], in_=band[:, b, :], pattern=[[1, SPAN]], compare_op=ALU.is_ge,
                fill=MASKED, base=0, channel_multiplier=-1,
            )
            nc.gpsimd.affine_select(
                out=band[:, b, :], in_=band[:, b, :], pattern=[[-1, SPAN]], compare_op=ALU.is_ge,
                fill=MASKED, base=2 * REACH, channel_multiplier=1,
            )
        nc.gpsimd.memset(band[:, 0, 0:REACH], MASKED)
        nc.gpsimd.memset(band[:, BLOCKS - 1, SPAN - REACH : SPAN], MASKED)

        def inside(b):
            return max(REACH - b * P, 0), min(SEQ_LEN + REACH - b * P, SPAN)

        x_pad = held.tile([P, CHUNKS, PADDED], BF16, name="x_pad")
        nc.gpsimd.memset(x_pad[:, :, 0:REACH], 0.0)
        nc.gpsimd.memset(x_pad[:, :, PADDED - REACH : PADDED], 0.0)
        value_blocks = PADDED // P
        values = held.tile([P, value_blocks, EMBED], BF16, name="values")
        ctx = held.tile([P, HEADS, TOKENS], BF16, name="ctx")
        prob = [held.tile([P, PAIR, SPAN], BF16, name=f"prob{slot}") for slot in range(PROB_RING)]
        for slot in range(PROB_RING):
            nc.gpsimd.memset(prob[slot][:], 0.0)

        query, keys = {}, {}
        expo, total = {}, {}
        prob_t = {}
        ctx_ps = {}

        def gather(s, c):
            piece = offsets[:, s * (SEQ_LEN // 16) : (s + 1) * (SEQ_LEN // 16)]
            picked = work.tile([P, SEQ_LEN], F32, name="picked")
            nc.scalar.activation(picked[:], table[c][:].indirect(piece), ACT.Copy)
            nc.vector.tensor_copy(x_pad[:, c, REACH + s * SEQ_LEN : REACH + (s + 1) * SEQ_LEN], picked[:])

        def project(weights, m, moving):
            proj_ps = psum.tile([P, SEQ_LEN], F32, name="proj_ps", bufs=3)
            for c in range(CHUNKS):
                nc.tensor.matmul(
                    proj_ps[:], weights[:, c, m * P : (m + 1) * P], moving[:, c, :],
                    start=(c == 0), stop=(c == CHUNKS - 1),
                )
            return proj_ps

        def x_of(s):
            return x_pad[:, :, REACH + s * SEQ_LEN : REACH + (s + 1) * SEQ_LEN]

        def project_query(s, h):
            if h == 0:
                query[s] = work.tile([P, HEADS, SEQ_LEN], BF16, name="query")
            nc.vector.tensor_scalar(
                query[s][:, h, :], project(wq_sb, h, x_of(s))[:], bq_sb[:, h : h + 1], HEAD_DIM ** -0.5,
                op0=ALU.add, op1=ALU.mult,
            )

        def project_key(s, h, on_scalar):
            if h == 0:
                keys[s] = work.tile([P, HEADS, SEQ_LEN], BF16, name="keys")
            if on_scalar:
                nc.scalar.copy(keys[s][:, h, :], project(wk_sb, h, x_of(s))[:])
            else:
                nc.vector.tensor_copy(keys[s][:, h, :], project(wk_sb, h, x_of(s))[:])

        def project_values(g, count, on_scalar):
            value_ps = psum.tile([P, PAIR, EMBED], F32, name="value_ps", tag="proj_ps", bufs=3)
            for k in range(count):
                for c in range(CHUNKS):
                    nc.tensor.matmul(
                        value_ps[:, k, :], x_pad[:, c, (g + k) * P : (g + k + 1) * P], wv_sb[:, c, :],
                        start=(c == 0), stop=(c == CHUNKS - 1),
                    )
            if on_scalar:
                nc.scalar.copy(values[:, g : g + count, :], value_ps[:, 0:count, :])
            else:
                nc.vector.tensor_copy(values[:, g : g + count, :], value_ps[:, 0:count, :])

        def project_out(s, m, on_scalar):
            out_ps = project(wo_sb, m, ctx[:, :, s * SEQ_LEN : (s + 1) * SEQ_LEN])
            out_sb = work.tile([P, SEQ_LEN], F32, name="out_sb")
            if on_scalar:
                nc.scalar.activation(out_sb[:], out_ps[:], ACT.Identity, bias=bo_sb[:, m : m + 1], scale=1.0)
            else:
                nc.vector.tensor_scalar_add(out_sb[:], out_ps[:], bo_sb[:, m : m + 1])
            nc.sync.dma_start(out[m * P : (m + 1) * P, s * SEQ_LEN : (s + 1) * SEQ_LEN], out_sb[:])

        def place(u):
            return u // UNITS_PER_SEQ, (u % UNITS_PER_SEQ) // 2, PAIR * (u % 2)

        def exponentials(u):
            s, h, first = place(u)
            score_ps = psum.tile([P, PAIR, SPAN], F32, name="score_ps")
            nc.tensor.matmul(score_ps[:], ident[:], band[:, first : first + PAIR, :], start=True, stop=False)
            for k in range(PAIR):
                b = first + k
                near, far = inside(b)
                nc.tensor.matmul(
                    score_ps[:, k, near:far], query[s][:, h, b * P : (b + 1) * P],
                    keys[s][:, h, b * P - REACH + near : b * P - REACH + far], start=False, stop=(k == PAIR - 1),
                )
            neg_max = stats.tile([P, PAIR], F32, name="neg_max")
            nc.vector.tensor_reduce(
                out=neg_max[:], in_=score_ps[:], axis=mybir.AxisListType.X, op=ALU.max, negate=True
            )
            expo[u] = work.tile([P, PAIR, SPAN], F32, name="expo")
            total[u] = stats.tile([P, PAIR], F32, name="total")
            for k in range(PAIR):
                near, far = inside(first + k)
                nc.scalar.activation(
                    expo[u][:, k, near:far], score_ps[:, k, near:far], ACT.Exp,
                    bias=neg_max[:, k : k + 1], scale=1.0, accum_out=total[u][:, k : k + 1],
                )

        def normalise(u):
            first = place(u)[2]
            inverse = stats.tile([P, PAIR], F32, name="inverse")
            nc.vector.reciprocal(inverse[:], total[u][:])
            for k in range(PAIR):
                near, far = inside(first + k)
                nc.gpsimd.tensor_scalar(
                    prob[u % PROB_RING][:, k, near:far], expo[u][:, k, near:far], inverse[:, k : k + 1], 0.0,
                    op0=ALU.mult, op1=ALU.add,
                )

        def flip(u):
            prob_t_ps = psum.tile([P, 2 * PAIR, P], BF16, name="prob_t_ps", bufs=1)
            for k in range(PAIR):
                for half in range(2):
                    nc.tensor.transpose(
                        prob_t_ps[:, 2 * k + half, :], prob[u % PROB_RING][:, k, half * P : (half + 1) * P],
                        ident[:],
                    )
            prob_t[u] = work.tile([P, 2 * PAIR, P], BF16, name="prob_t")
            nc.vector.tensor_copy(prob_t[u][:], prob_t_ps[:])

        def weigh(u):
            s, h, first = place(u)
            if first == 0:
                ctx_ps[s, h] = psum.tile([P, SEQ_LEN], F32, name="ctx_ps")
            g = BLOCKS * s + first
            nc.tensor.matmul(
                ctx_ps[s, h][:, first * P : (first + 2) * P], values[:, g + 1, h * P : (h + 1) * P],
                prob_t[u][:, 1:3, :], start=True, stop=False,
            )
            nc.tensor.matmul(
                ctx_ps[s, h][:, first * P : (first + 1) * P], values[:, g, h * P : (h + 1) * P],
                prob_t[u][:, 0, :], start=False, stop=False,
            )
            nc.tensor.matmul(
                ctx_ps[s, h][:, (first + 1) * P : (first + 2) * P], values[:, g + 2, h * P : (h + 1) * P],
                prob_t[u][:, 3, :], start=False, stop=True,
            )
            if first + PAIR == BLOCKS:
                nc.scalar.activation(
                    ctx[:, h, s * SEQ_LEN : (s + 1) * SEQ_LEN], ctx_ps[s, h][:], ACT.Identity,
                    bias=bv_sb[:, h : h + 1], scale=1.0,
                )

        def looks_up(u):
            return u % 2 == 1 and u // UNITS_PER_SEQ + LOOK_AHEAD < SEQS

        def product_before_attention(s, n, on_scalar):
            if n >= 2 * HEADS:
                project_values(BLOCKS * s + PAIR * (n - 2 * HEADS), PAIR, on_scalar)
            elif n % 2 == 0:
                project_query(s, n // 2)
            else:
                project_key(s, n // 2, on_scalar)

        def side_product(u, part):
            s, quarter = divmod(u, UNITS_PER_SEQ)
            on_scalar = part == 1 and not looks_up(u)
            if u >= LAST_SEQ_START:
                if u == LAST_SEQ_START and part == 0:
                    project_values(value_blocks - 1, 1, on_scalar)
                project_out(SEQS - 1 - OUT_LAG + u - LAST_SEQ_START, part, on_scalar)
            elif quarter % 2 == 0:
                product_before_attention(s + 1, BEFORE_ATTENTION // 2 * (quarter // 2) + part, on_scalar)
            elif part == 0:
                product_before_attention(s + 1, BEFORE_ATTENTION // 2 * (quarter // 2) + 2, on_scalar)
            elif s >= OUT_LAG:
                project_out(s - OUT_LAG, quarter // 2, on_scalar)

        for c in range(CHUNKS):
            for s in range(LOOK_AHEAD):
                gather(s, c)
        for n in range(BEFORE_ATTENTION):
            product_before_attention(0, n, on_scalar=(n % 2 == 1))

        for u in range(UNITS + WEIGH_LAG):
            if u < UNITS:
                if looks_up(u):
                    gather(u // UNITS_PER_SEQ + LOOK_AHEAD, (u % UNITS_PER_SEQ) // 2)
                exponentials(u)
            if FLIP_LAG <= u < UNITS + FLIP_LAG:
                flip(u - FLIP_LAG)
            side_product(u, 0)
            if u < UNITS:
                normalise(u)
            side_product(u, 1)
            if u >= WEIGH_LAG:
                weigh(u - WEIGH_LAG)
        for m in range(CHUNKS):
            project_out(SEQS - 1, m, on_scalar=(m == 1))
